import numpy as np
import ml_dtypes


def mxq(x, axis, fmt="e4m3"):
    dtype, down = {"e4m3": (ml_dtypes.float8_e4m3fn, 7), "e5m2": (ml_dtypes.float8_e5m2, 14)}[fmt]
    v = np.moveaxis(np.asarray(x, np.float32).astype(ml_dtypes.bfloat16).astype(np.float64), axis, -1)
    blocks = v.reshape(v.shape[:-1] + (-1, 32))
    amax = np.abs(blocks).max(-1, keepdims=True)
    byte = np.maximum(np.where(amax > 0, np.frexp(amax)[1] - 1 + 127, 0) - down, 1)
    scale = np.exp2(byte - 127.0)
    codes = (blocks / scale).astype(np.float32).astype(dtype).astype(np.float64)
    return np.moveaxis((codes * scale).reshape(v.shape), -1, axis)


WIDE = False


def mx_kscale(k):
    if not WIDE:
        return np.ones(k)
    levels = np.array([10, -10, 5, -5, 0])
    if k % 512:
        return np.exp2(np.random.permutation(np.resize(levels, k // 32))).repeat(32)
    a = np.empty((k // 512, 16))
    for p in range(k // 512):
        a[p, :8] = np.random.permutation(np.resize(levels, 8))
        for g in range(8):
            far = levels[np.abs(levels - a[p, g]) >= 10]
            a[p, g + 8] = far[np.random.randint(len(far))]
    return np.exp2(a.ravel()).repeat(32)


BF16 = ml_dtypes.bfloat16


def bf(x):
    return np.asarray(x, np.float32).astype(BF16)


def f64(x):
    return np.asarray(x).astype(np.float64)


B, CIN, R, COUT, H, W, D, KS = 1, 512, 512, 512, 8, 16, 16, 3
P = H * W * D
PAD = (KS - 1) // 2


def slice_in_dim(t, a, b, axis):
    idx = [slice(None)] * t.ndim
    idx[axis] = slice(a, b)
    return t[tuple(idx)]


def axis_contract(t, U, axis):
    L = t.shape[axis] - (KS - 1)
    rshape = (1, U.shape[1], 1, 1, 1)
    acc = slice_in_dim(t, 0, L, axis) * U[0].reshape(rshape)
    for k in range(1, KS):
        acc = acc + slice_in_dim(t, k, k + L, axis) * U[k].reshape(rshape)
    return acc


def setup_inputs():
    s, t = mx_kscale(CIN), mx_kscale(R)
    return {"x": bf(np.random.standard_normal((B, CIN, H, W, D)) * s[None, :, None, None, None]),
            "U_kh": bf(np.random.standard_normal((KS, R)) / np.sqrt(KS)),
            "U_kw": bf(np.random.standard_normal((KS, R)) / np.sqrt(KS)),
            "U_kd": bf(np.random.standard_normal((KS, R)) / np.sqrt(KS)),
            "U_c_in": bf(np.random.standard_normal((CIN, R)) / np.sqrt(CIN) / s[:, None] * t[None, :]),
            "U_c_out": bf(np.random.standard_normal((R, COUT)) / np.sqrt(R) / t[:, None]),
            "bias": bf(np.random.standard_normal(COUT) * 0.5)}


def reference(x, U_kh, U_kw, U_kd, U_c_in, U_c_out, bias):
    xq = mxq(f64(x), 1, "e4m3").reshape(B, CIN, P)
    y = f64(bf(mxq(f64(U_c_in), 0, "e4m3").T @ xq)).reshape(B, R, H, W, D)
    y = np.pad(y, ((0, 0), (0, 0), (PAD, PAD), (PAD, PAD), (PAD, PAD)))
    y = axis_contract(y, f64(U_kh), 2)
    y = axis_contract(y, f64(U_kw), 3)
    y = axis_contract(y, f64(U_kd), 4)
    out = (mxq(f64(U_c_out), 0, "e4m3").T @ mxq(y, 1, "e4m3").reshape(B, R, P)).reshape(B, COUT, H, W, D)
    return out + f64(bias)[None, :, None, None, None]

@@ -1,0 +1,341 @@
+from contextlib import ExitStack
+
+import concourse.mybir as mybir
+from concourse.masks import make_identity
+
+F32 = mybir.dt.float32
+BF16 = mybir.dt.bfloat16
+U32 = mybir.dt.uint32
+U8 = mybir.dt.uint8
+FP8X4 = mybir.dt.float8_e4m3fn_x4
+MULT = mybir.AluOpType.mult
+ADD = mybir.AluOpType.add
+IDENT = mybir.ActivationFunctionType.Identity
+
+BANK_DT = BF16
+
+P = 128
+PACK = 4
+CIN, RANK, COUT = 512, 512, 512
+H, W, D = 8, 16, 16
+POS = H * W * D
+SLAB = W * D
+CHUNK = 2 * SLAB
+NCHUNK = POS // CHUNK
+Y1_PITCH = SLAB + D
+Y1_SIZE = (H + 1) * Y1_PITCH
+ROWS = CHUNK // D
+Y2_PITCH = D + 4
+Y2_SIZE = (ROWS + 1) * Y2_PITCH
+FH, FW, FD = 0, 1, 2
+T_PE = 3
+T_VE = (0, 1, 2)
+
+FLOPS = 2 * POS * RANK * (CIN + COUT) + 3 * 5 * POS * RANK
+
+
+def tile_lowrankconv3d_kernel(tc, x, U_kh, U_kw, U_kd, U_c_in, U_c_out, bias, out):
+    nc = tc.nc
+    x_rows = x.rearrange("b c h w d -> (b c) (h w d)").rearrange("(p j) n -> p j n", j=PACK)
+    out_rows = out.rearrange("b c h w d -> (b c) (h w d)").rearrange("(p m) n -> p m n", m=PACK)
+
+    with ExitStack() as ctx:
+        keep = ctx.enter_context(tc.tile_pool(name="keep", bufs=1))
+        stage = ctx.enter_context(tc.tile_pool(name="stage", bufs=16))
+        psum = ctx.enter_context(tc.psum_pool(name="psum", bufs=8))
+        ctx.enter_context(tc.manual_schedule())
+
+        def keep_tile(name, shape, dtype):
+            return keep.tile(shape, dtype, name=name, tag=name, align_bytes=64)
+
+        taps_bf = [keep_tile("taps_bf%d" % f, [P, 3, PACK], BF16) for f in range(3)]
+        bias_bf = keep_tile("bias_bf", [P, PACK], BF16)
+        taps = keep_tile("taps", [P, 3, 3, PACK], F32)
+        bias_f = keep_tile("bias_f", [P, PACK], F32)
+        w_raw = [keep_tile("w_raw%d" % s, [P, PACK, 512], BF16) for s in range(2)]
+        w_grp = [keep_tile("w_grp%d" % s, [P, 2048], BF16) for s in range(2)]
+        w_codes = [keep_tile("w_codes%d" % s, [P, 512], U32) for s in range(2)]
+        w_scales = [keep_tile("w_scales%d" % s, [P, 512], U8) for s in range(2)]
+        x_raw = [keep_tile("x_raw%d" % n, [P, PACK, CHUNK], BF16) for n in range(NCHUNK)]
+        x_grp = [keep_tile("x_grp%d" % b, [P, CHUNK, PACK], BF16) for b in range(2)]
+        x_codes = [keep_tile("x_codes%d" % n, [P, CHUNK], U32) for n in range(NCHUNK)]
+        x_scales = [keep_tile("x_scales%d" % n, [P, CHUNK], U8) for n in range(NCHUNK)]
+        y1 = [keep_tile("y1_%d" % t, [P, Y1_SIZE], F32) for t in range(PACK)]
+        y2 = [[keep_tile("y2_%d_%d" % (t, b), [P, Y2_SIZE], F32) for b in range(2)] for t in range(PACK)]
+        y2d = [[keep_tile("y2d_%d_%d" % (t, b), [P, CHUNK], F32) for b in range(2)] for t in range(PACK)]
+        y3 = [keep_tile("y3_%d" % b, [P, PACK, CHUNK], BF16) for b in range(2)]
+        y3_grp = [keep_tile("y3_grp%d" % b, [P, CHUNK, PACK], BF16) for b in range(2)]
+        y3_codes = [keep_tile("y3_codes%d" % b, [P, CHUNK], U32) for b in range(2)]
+        y3_scales = [keep_tile("y3_scales%d" % b, [P, CHUNK], U8) for b in range(2)]
+        ident = keep_tile("ident", [P, P], F32)
+        diag = [keep_tile("diag%d" % k, [P, P], BANK_DT) for k in range(3)]
+        y0 = keep_tile("y0", [P, (H + 2) * SLAB], BANK_DT)
+        warm = keep_tile("warm", [P, 2], F32)
+        banks = {}
+
+        def tap(f, k, t):
+            return taps[:, f, k, t : t + 1]
+
+        def slab(t, h, count=1):
+            start = D + h * Y1_PITCH
+            if count == 1:
+                return y1[t][:, start : start + SLAB]
+            return y1[t][:, start : start + count * Y1_PITCH].rearrange("p (s c) -> p s c", c=Y1_PITCH)[:, :, 0:SLAB]
+
+        def y1_window(t, n, shift):
+            start = D + 2 * n * Y1_PITCH + shift * D
+            two = y1[t][:, start : start + 2 * Y1_PITCH].rearrange("p (s c) -> p s c", c=Y1_PITCH)[:, :, 0:SLAB]
+            return two.rearrange("p s (w d) -> p s w d", d=D)
+
+        def y2_window(t, n, shift, rows=slice(0, ROWS)):
+            start = 4 + shift
+            view = y2[t][n % 2][:, start : start + ROWS * Y2_PITCH].rearrange("p (r c) -> p r c", c=Y2_PITCH)
+            return view[:, rows, 0:D]
+
+        def y2_rows4(t, n):
+            return y2_window(t, n, 0).rearrange("p (s w) d -> p s w d", s=2)
+
+        def as_rows(ap, rows=slice(0, ROWS)):
+            return ap.rearrange("p (r d) -> p r d", d=D)[:, rows, :]
+
+        def scaled(out_ap, in_ap, scale_ap):
+            nc.scalar.activation(out=out_ap, in_=in_ap, func=IDENT, bias=0.0, scale=scale_ap)
+
+        def mac(out_ap, in_ap, scale_ap, acc_ap):
+            nc.vector.scalar_tensor_tensor(out=out_ap, in0=in_ap, scalar=scale_ap, in1=acc_ap, op0=MULT, op1=ADD)
+
+        def copy_on(engine, out_ap, in_ap):
+            if engine == "V":
+                nc.vector.tensor_copy(out=out_ap, in_=in_ap)
+            elif engine == "S":
+                nc.scalar.copy(out=out_ap, in_=in_ap)
+            else:
+                nc.gpsimd.tensor_scalar(out=out_ap, in0=in_ap, scalar1=1.0, scalar2=0.0, op0=MULT, op1=ADD)
+
+        def group_weight(engine, s, t0, t1):
+            dst = w_grp[s].rearrange("p (t m j) -> p t m j", t=PACK, j=PACK)
+            src = w_raw[s].rearrange("p j (m t) -> p t m j", t=PACK)
+            copy_on(engine, dst[:, t0:t1], src[:, t0:t1])
+
+        def group_x(engine, n, c0, c1):
+            copy_on(engine, x_grp[n % 2][:, c0:c1, :], x_raw[n].rearrange("p j c -> p c j")[:, c0:c1, :])
+
+        def group_y3(engine, n, c0, c1):
+            copy_on(engine, y3_grp[n % 2][:, c0:c1, :], y3[n % 2].rearrange("p t c -> p c t")[:, c0:c1, :])
+
+        def quantize(codes, scales, grouped):
+            nc.vector.quantize_mx(out=codes.bitcast(FP8X4), scales=scales, in_=grouped)
+
+        def quantize_x(n):
+            quantize(x_codes[n], x_scales[n], x_grp[n % 2].rearrange("p c j -> p (c j)"))
+
+        def quantize_y3(n, c0=0, c1=CHUNK):
+            grouped = y3_grp[n % 2].rearrange("p c j -> p (c j)")
+            quantize(y3_codes[n % 2][:, c0:c1], y3_scales[n % 2][:, c0:c1], grouped[:, PACK * c0 : PACK * c1])
+
+        def product(dtype, s, m, codes, scales):
+            bank = psum.tile([P, codes.shape[1]], dtype, name="bank", tag="bank")
+            cols = slice(m * P, (m + 1) * P)
+            nc.tensor.matmul_mx(
+                out=bank,
+                lhsT=w_codes[s][:, cols].bitcast(FP8X4),
+                lhsT_scale=w_scales[s][:, cols],
+                rhs=codes.bitcast(FP8X4),
+                rhs_scale=scales,
+                start=True,
+                stop=True,
+            )
+            return bank
+
+        def first_product(n):
+            for t in T_VE + (T_PE,) if n == 0 else (T_PE,) + T_VE:
+                banks[(t, n)] = product(BANK_DT, 0, t, x_codes[n], x_scales[n])
+
+        def h_copy_in(n):
+            nc.scalar.copy(out=y0[:, (2 * n + 1) * SLAB : (2 * n + 3) * SLAB], in_=banks[(T_PE, n)])
+
+        def h_tensor(n):
+            bank = psum.tile([P, CHUNK], F32, name="bank", tag="bank")
+            for k in range(3):
+                nc.tensor.matmul(out=bank, lhsT=diag[k], rhs=y0[:, (2 * n + k) * SLAB : (2 * n + k + 2) * SLAB], start=(k == 0), stop=(k == 2))
+            banks[("h", n)] = bank
+
+        def h_copy_out(n):
+            nc.scalar.copy(out=slab(T_PE, 2 * n, 2), in_=banks[("h", n)].rearrange("p (s c) -> p s c", c=SLAB))
+
+        def h_scalar(t, n):
+            bank = banks[(t, n)]
+            scaled(slab(t, 2 * n + 1), bank[:, SLAB:CHUNK], tap(FH, 1, t))
+            if n < NCHUNK - 1:
+                scaled(slab(t, 2 * n + 2), bank[:, SLAB:CHUNK], tap(FH, 0, t))
+
+        def h_vector_first_a(t):
+            nc.vector.tensor_scalar(out=slab(t, 0), in0=banks[(t, 0)][:, 0:SLAB], scalar1=tap(FH, 1, t), scalar2=None, op0=MULT)
+
+        def h_vector_first_b(t):
+            mac(slab(t, 0), banks[(t, 0)][:, SLAB:CHUNK], tap(FH, 2, t), slab(t, 0))
+
+        def h_vector_a(t, n):
+            bank = banks[(t, n)]
+            if n > 0:
+                mac(slab(t, 2 * n), bank[:, 0:SLAB], tap(FH, 1, t), slab(t, 2 * n))
+            mac(slab(t, 2 * n + 1), bank[:, 0:SLAB], tap(FH, 0, t), slab(t, 2 * n + 1))
+
+        def h_vector_b(t, n):
+            both = slab(t, 2 * n - 1, 2)
+            mac(both, banks[(t, n)].rearrange("p (s c) -> p s c", c=SLAB), tap(FH, 2, t), both)
+
+        def w_scalar(t, n):
+            scaled(y2_rows4(t, n), y1_window(t, n, 0), tap(FW, 1, t))
+
+        def w_vector_a(t, n):
+            mac(y2_rows4(t, n), y1_window(t, n, -1), tap(FW, 0, t), y2_rows4(t, n))
+
+        def w_vector_b(t, n):
+            mac(y2_rows4(t, n), y1_window(t, n, 1), tap(FW, 2, t), y2_rows4(t, n))
+
+        def d_scalar(t, n, rows=slice(0, ROWS)):
+            scaled(as_rows(y2d[t][n % 2], rows), y2_window(t, n, -1, rows), tap(FD, 0, t))
+
+        def d_vector_a(t, n, rows=slice(0, ROWS)):
+            acc = as_rows(y2d[t][n % 2], rows)
+            mac(acc, y2_window(t, n, 1, rows), tap(FD, 2, t), acc)
+
+        def d_vector_b(t, n, rows=slice(0, ROWS)):
+            mac(as_rows(y3[n % 2][:, t, :], rows), y2_window(t, n, 0, rows), tap(FD, 1, t), as_rows(y2d[t][n % 2], rows))
+
+        def second_product(n, c0=0, c1=CHUNK):
+            for m in range(PACK):
+                banks[("out", m, n, c0)] = product(F32, 1, m, y3_codes[n % 2][:, c0:c1], y3_scales[n % 2][:, c0:c1])
+
+        def store(engine, m, n, c0=0, c1=CHUNK):
+            res = stage.tile([P, c1 - c0], F32, name="res", tag="res")
+            if engine == "S":
+                nc.scalar.activation(out=res, in_=banks[("out", m, n, c0)], func=IDENT, bias=bias_f[:, m : m + 1], scale=1.0)
+            else:
+                nc.vector.tensor_scalar(out=res, in0=banks[("out", m, n, c0)], scalar1=bias_f[:, m : m + 1], scalar2=None, op0=ADD)
+            nc.sync.dma_start(out=out_rows[:, m, n * CHUNK + c0 : n * CHUNK + c1], in_=res)
+
+        def each(steps, ts, *args):
+            for step in steps:
+                for t in ts:
+                    step(t, *args)
+
+        nc.gpsimd.memset(warm, 0.0)
+        for t in range(PACK):
+            nc.gpsimd.memset(y1[t].rearrange("p (s c) -> p s c", c=Y1_PITCH)[:, :, 0:D], 0.0)
+            for b in range(2):
+                nc.gpsimd.memset(y2[t][b].rearrange("p (r c) -> p r c", c=Y2_PITCH)[:, :, 0:4], 0.0)
+
+        for f, u in enumerate((U_kh, U_kw, U_kd)):
+            nc.scalar.dma_start(out=taps_bf[f], in_=u.rearrange("k (p t) -> p k t", t=PACK))
+        nc.scalar.dma_start(out=bias_bf, in_=bias.rearrange("(p m) -> p m", m=PACK))
+        nc.scalar.activation(out=warm[:, 1:2], in_=warm[:, 0:1], func=IDENT, bias=0.0, scale=1.0)
+        nc.sync.dma_start(out=w_raw[0], in_=U_c_in.rearrange("(p j) r -> p j r", j=PACK))
+        for n in range(NCHUNK):
+            nc.sync.dma_start(out=x_raw[n], in_=x_rows[:, :, n * CHUNK : (n + 1) * CHUNK])
+        nc.sync.dma_start(out=w_raw[1], in_=U_c_out.rearrange("(p j) r -> p j r", j=PACK))
+
+        nc.gpsimd.memset(y0[:, 0:SLAB], 0.0)
+        nc.gpsimd.memset(y0[:, (H + 1) * SLAB : (H + 2) * SLAB], 0.0)
+        make_identity(nc, ident)
+        for f in range(3):
+            nc.vector.tensor_copy(out=taps[:, f], in_=taps_bf[f])
+        nc.vector.tensor_copy(out=bias_f, in_=bias_bf)
+        for k in range(3):
+            scaled(diag[k], ident, tap(FH, k, T_PE))
+
+        group_weight("V", 0, 0, PACK)
+        group_x("S", 0, SLAB, CHUNK)
+        group_x("V", 0, 0, SLAB)
+        quantize(w_codes[0], w_scales[0], w_grp[0])
+        quantize_x(0)
+        first_product(0)
+        group_x("S", 1, SLAB, CHUNK)
+        group_x("V", 1, 0, SLAB)
+        quantize_x(1)
+        first_product(1)
+        for n in (3, 2):
+            group_x("G", n, 0, SLAB)
+            group_x("G", n, SLAB, CHUNK)
+
+        each([h_scalar], T_VE, 0)
+        for t in T_VE:
+            h_vector_first_a(t)
+            h_vector_a(t, 0)
+            h_vector_first_b(t)
+        h_scalar(0, 1)
+        h_copy_in(0)
+        h_copy_in(1)
+        h_tensor(0)
+        each([h_scalar], (1, 2), 1)
+
+        for n in range(NCHUNK - 1):
+            for t in T_VE:
+                h_vector_a(t, n + 1)
+                h_vector_b(t, n + 1)
+            each([w_scalar], T_VE, n)
+            if n + 2 < NCHUNK:
+                quantize_x(n + 2)
+                first_product(n + 2)
+            h_copy_out(n)
+            w_scalar(T_PE, n)
+            each([w_vector_a, w_vector_b], (0, 1), n)
+            each([d_scalar], (0, 1), n)
+            if n + 2 < NCHUNK:
+                h_copy_in(n + 2)
+            h_tensor(n + 1)
+            if n == 1:
+                quantize(w_codes[1], w_scales[1], w_grp[1])
+            if n >= 1:
+                quantize_y3(n - 1)
+                second_product(n - 1)
+            each([w_vector_a, w_vector_b], (2, 3), n)
+            each([d_scalar], (2, 3), n)
+            each([d_vector_a, d_vector_b], (0, 1), n)
+            if n + 2 < NCHUNK:
+                each([h_scalar], T_VE, n + 2)
+            else:
+                each([w_scalar], T_VE, n + 1)
+                h_copy_out(n + 1)
+                w_scalar(T_PE, n + 1)
+            for m in range(PACK):
+                if n == 0:
+                    group_weight("S", 1, m, m + 1)
+                else:
+                    store("S", m, n - 1)
+            each([d_vector_a, d_vector_b], (2, 3), n)
+            if n + 2 < NCHUNK:
+                group_y3("G", n, 0, 192)
+                group_y3("G", n, 192, 384)
+                group_y3("S", n, 384, CHUNK)
+
+        n = NCHUNK - 1
+        top, bottom = slice(0, W), slice(W, ROWS)
+        for q in range(4):
+            group_y3("S", n - 1, q * SLAB // 2, (q + 1) * SLAB // 2)
+        each([w_vector_a, w_vector_b], (0, 1), n)
+        each([d_scalar], (0, 1), n, top)
+        each([w_vector_a, w_vector_b], (2, 3), n)
+        quantize_y3(n - 1)
+        second_product(n - 1)
+        each([d_scalar], (2, 3), n, top)
+        each([d_vector_a, d_vector_b], (0, 1), n, top)
+        each([d_scalar], (0, 1, 2, 3), n, bottom)
+        each([d_vector_a, d_vector_b], (2, 3), n, top)
+        group_y3("S", n, 0, SLAB // 2)
+        group_y3("S", n, SLAB // 2, SLAB)
+        each([d_vector_a, d_vector_b], (0, 1), n, bottom)
+        for m in range(PACK):
+            store("S", m, n - 1)
+        each([d_vector_a], (2, 3), n, bottom)
+        quantize_y3(n, 0, SLAB)
+        second_product(n, 0, SLAB)
+        each([d_vector_b], (2, 3), n, bottom)
+        for m in range(PACK):
+            store("S", m, n, 0, SLAB)
+        group_y3("V", n, SLAB, CHUNK)
+        quantize_y3(n, SLAB, CHUNK)
+        second_product(n, SLAB, CHUNK)
+        for m in range(PACK):
+            store("V" if m % 2 == 0 else "S", m, n, SLAB, CHUNK)

@@ -25,11 +25,13 @@ NCHUNK = POS // CHUNK
 Y1_PITCH = SLAB + D
 Y1_SIZE = (H + 1) * Y1_PITCH
 ROWS = CHUNK // D
-Y2_PITCH = D + 4
+Y2_PAD = 4
+Y2_PITCH = D + Y2_PAD
 Y2_SIZE = (ROWS + 1) * Y2_PITCH
 FH, FW, FD = 0, 1, 2
-T_PE = 3
 T_VE = (0, 1, 2)
+T_PE = 3
+G_SHARE = 384
 
 FLOPS = 2 * POS * RANK * (CIN + COUT) + 3 * 5 * POS * RANK
 
@@ -48,55 +50,58 @@ def tile_lowrankconv3d_kernel(tc, x, U_kh, U_kw, U_kd, U_c_in, U_c_out, bias, ou
         def keep_tile(name, shape, dtype):
             return keep.tile(shape, dtype, name=name, tag=name, align_bytes=64)
 
+        warm = keep_tile("warm", [P, 2], F32)
         taps_bf = [keep_tile("taps_bf%d" % f, [P, 3, PACK], BF16) for f in range(3)]
         bias_bf = keep_tile("bias_bf", [P, PACK], BF16)
         taps = keep_tile("taps", [P, 3, 3, PACK], F32)
         bias_f = keep_tile("bias_f", [P, PACK], F32)
+        ident = keep_tile("ident", [P, P], F32)
+        diag = [keep_tile("diag%d" % k, [P, P], BANK_DT) for k in range(3)]
         w_raw = [keep_tile("w_raw%d" % s, [P, PACK, 512], BF16) for s in range(2)]
-        w_grp = [keep_tile("w_grp%d" % s, [P, 2048], BF16) for s in range(2)]
+        w_grp = [keep_tile("w_grp%d" % s, [P, PACK * 512], BF16) for s in range(2)]
         w_codes = [keep_tile("w_codes%d" % s, [P, 512], U32) for s in range(2)]
         w_scales = [keep_tile("w_scales%d" % s, [P, 512], U8) for s in range(2)]
         x_raw = [keep_tile("x_raw%d" % n, [P, PACK, CHUNK], BF16) for n in range(NCHUNK)]
         x_grp = [keep_tile("x_grp%d" % b, [P, CHUNK, PACK], BF16) for b in range(2)]
         x_codes = [keep_tile("x_codes%d" % n, [P, CHUNK], U32) for n in range(NCHUNK)]
         x_scales = [keep_tile("x_scales%d" % n, [P, CHUNK], U8) for n in range(NCHUNK)]
+        y0_pe = keep_tile("y0_pe", [P, (H + 2) * SLAB], BANK_DT)
         y1 = [keep_tile("y1_%d" % t, [P, Y1_SIZE], F32) for t in range(PACK)]
         y2 = [[keep_tile("y2_%d_%d" % (t, b), [P, Y2_SIZE], F32) for b in range(2)] for t in range(PACK)]
-        y2d = [[keep_tile("y2d_%d_%d" % (t, b), [P, CHUNK], F32) for b in range(2)] for t in range(PACK)]
+        acc = [[keep_tile("acc_%d_%d" % (t, b), [P, CHUNK], F32) for b in range(2)] for t in range(PACK)]
         y3 = [keep_tile("y3_%d" % b, [P, PACK, CHUNK], BF16) for b in range(2)]
         y3_grp = [keep_tile("y3_grp%d" % b, [P, CHUNK, PACK], BF16) for b in range(2)]
         y3_codes = [keep_tile("y3_codes%d" % b, [P, CHUNK], U32) for b in range(2)]
         y3_scales = [keep_tile("y3_scales%d" % b, [P, CHUNK], U8) for b in range(2)]
-        ident = keep_tile("ident", [P, P], F32)
-        diag = [keep_tile("diag%d" % k, [P, P], BANK_DT) for k in range(3)]
-        y0 = keep_tile("y0", [P, (H + 2) * SLAB], BANK_DT)
-        warm = keep_tile("warm", [P, 2], F32)
         banks = {}
 
         def tap(f, k, t):
             return taps[:, f, k, t : t + 1]
 
-        def slab(t, h, count=1):
+        def slabs(t, h, count):
             start = D + h * Y1_PITCH
-            if count == 1:
-                return y1[t][:, start : start + SLAB]
             return y1[t][:, start : start + count * Y1_PITCH].rearrange("p (s c) -> p s c", c=Y1_PITCH)[:, :, 0:SLAB]
+
+        def bank_slabs(bank):
+            return bank.rearrange("p (s c) -> p s c", c=SLAB)
 
         def y1_window(t, n, shift):
             start = D + 2 * n * Y1_PITCH + shift * D
             two = y1[t][:, start : start + 2 * Y1_PITCH].rearrange("p (s c) -> p s c", c=Y1_PITCH)[:, :, 0:SLAB]
             return two.rearrange("p s (w d) -> p s w d", d=D)
 
-        def y2_window(t, n, shift, rows=slice(0, ROWS)):
-            start = 4 + shift
+        def y2_window(t, n, shift, rows):
+            start = Y2_PAD + shift
             view = y2[t][n % 2][:, start : start + ROWS * Y2_PITCH].rearrange("p (r c) -> p r c", c=Y2_PITCH)
             return view[:, rows, 0:D]
 
-        def y2_rows4(t, n):
-            return y2_window(t, n, 0).rearrange("p (s w) d -> p s w d", s=2)
+        def y2_chunk(t, n):
+            return y2_window(t, n, 0, ALL_ROWS).rearrange("p (s w) d -> p s w d", s=2)
 
-        def as_rows(ap, rows=slice(0, ROWS)):
+        def as_rows(ap, rows):
             return ap.rearrange("p (r d) -> p r d", d=D)[:, rows, :]
+
+        ALL_ROWS = slice(0, ROWS)
 
         def scaled(out_ap, in_ap, scale_ap):
             nc.scalar.activation(out=out_ap, in_=in_ap, func=IDENT, bias=0.0, scale=scale_ap)
@@ -126,6 +131,9 @@ def tile_lowrankconv3d_kernel(tc, x, U_kh, U_kw, U_kd, U_c_in, U_c_out, bias, ou
         def quantize(codes, scales, grouped):
             nc.vector.quantize_mx(out=codes.bitcast(FP8X4), scales=scales, in_=grouped)
 
+        def quantize_weight(s):
+            quantize(w_codes[s], w_scales[s], w_grp[s])
+
         def quantize_x(n):
             quantize(x_codes[n], x_scales[n], x_grp[n % 2].rearrange("p c j -> p (c j)"))
 
@@ -151,58 +159,58 @@ def tile_lowrankconv3d_kernel(tc, x, U_kh, U_kw, U_kd, U_c_in, U_c_out, bias, ou
             for t in T_VE + (T_PE,) if n == 0 else (T_PE,) + T_VE:
                 banks[(t, n)] = product(BANK_DT, 0, t, x_codes[n], x_scales[n])
 
+        def h_lower(t, n):
+            count = 2 if n < NCHUNK - 1 else 1
+            scaled(slabs(t, 2 * n + 1, count), bank_slabs(banks[(t, n)])[:, 0:count], tap(FH, 0, t))
+
+        def h_centre(t, n):
+            mac(slabs(t, 2 * n, 2), bank_slabs(banks[(t, n)]), tap(FH, 1, t), slabs(t, 2 * n, 2))
+
+        def h_upper(t, n):
+            first = 0 if n > 0 else 1
+            dst = slabs(t, 2 * n - 1 + first, 2 - first)
+            mac(dst, bank_slabs(banks[(t, n)])[:, first:2], tap(FH, 2, t), dst)
+
+        def h_vector(n):
+            for step in (h_centre, h_upper):
+                for t in T_VE:
+                    step(t, n)
+
         def h_copy_in(n):
-            nc.scalar.copy(out=y0[:, (2 * n + 1) * SLAB : (2 * n + 3) * SLAB], in_=banks[(T_PE, n)])
+            nc.scalar.copy(out=y0_pe[:, (2 * n + 1) * SLAB : (2 * n + 3) * SLAB], in_=banks[(T_PE, n)])
 
         def h_tensor(n):
             bank = psum.tile([P, CHUNK], F32, name="bank", tag="bank")
             for k in range(3):
-                nc.tensor.matmul(out=bank, lhsT=diag[k], rhs=y0[:, (2 * n + k) * SLAB : (2 * n + k + 2) * SLAB], start=(k == 0), stop=(k == 2))
+                moving = y0_pe[:, (2 * n + k) * SLAB : (2 * n + k + 2) * SLAB]
+                nc.tensor.matmul(out=bank, lhsT=diag[k], rhs=moving, start=(k == 0), stop=(k == 2))
             banks[("h", n)] = bank
 
         def h_copy_out(n):
-            nc.scalar.copy(out=slab(T_PE, 2 * n, 2), in_=banks[("h", n)].rearrange("p (s c) -> p s c", c=SLAB))
+            nc.scalar.copy(out=slabs(T_PE, 2 * n, 2), in_=bank_slabs(banks[("h", n)]))
 
-        def h_scalar(t, n):
-            bank = banks[(t, n)]
-            scaled(slab(t, 2 * n + 1), bank[:, SLAB:CHUNK], tap(FH, 1, t))
-            if n < NCHUNK - 1:
-                scaled(slab(t, 2 * n + 2), bank[:, SLAB:CHUNK], tap(FH, 0, t))
+        def w_centre(t, n):
+            scaled(y2_chunk(t, n), y1_window(t, n, 0), tap(FW, 1, t))
 
-        def h_vector_first_a(t):
-            nc.vector.tensor_scalar(out=slab(t, 0), in0=banks[(t, 0)][:, 0:SLAB], scalar1=tap(FH, 1, t), scalar2=None, op0=MULT)
+        def w_lower(t, n):
+            mac(y2_chunk(t, n), y1_window(t, n, -1), tap(FW, 0, t), y2_chunk(t, n))
 
-        def h_vector_first_b(t):
-            mac(slab(t, 0), banks[(t, 0)][:, SLAB:CHUNK], tap(FH, 2, t), slab(t, 0))
+        def w_upper(t, n):
+            mac(y2_chunk(t, n), y1_window(t, n, 1), tap(FW, 2, t), y2_chunk(t, n))
 
-        def h_vector_a(t, n):
-            bank = banks[(t, n)]
-            if n > 0:
-                mac(slab(t, 2 * n), bank[:, 0:SLAB], tap(FH, 1, t), slab(t, 2 * n))
-            mac(slab(t, 2 * n + 1), bank[:, 0:SLAB], tap(FH, 0, t), slab(t, 2 * n + 1))
+        def d_lower(t, n, rows=ALL_ROWS):
+            scaled(as_rows(acc[t][n % 2], rows), y2_window(t, n, -1, rows), tap(FD, 0, t))
 
-        def h_vector_b(t, n):
-            both = slab(t, 2 * n - 1, 2)
-            mac(both, banks[(t, n)].rearrange("p (s c) -> p s c", c=SLAB), tap(FH, 2, t), both)
+        def d_upper(t, n, rows=ALL_ROWS):
+            mac(as_rows(acc[t][n % 2], rows), y2_window(t, n, 1, rows), tap(FD, 2, t), as_rows(acc[t][n % 2], rows))
 
-        def w_scalar(t, n):
-            scaled(y2_rows4(t, n), y1_window(t, n, 0), tap(FW, 1, t))
+        def d_centre(t, n, rows=ALL_ROWS):
+            mac(as_rows(y3[n % 2][:, t, :], rows), y2_window(t, n, 0, rows), tap(FD, 1, t), as_rows(acc[t][n % 2], rows))
 
-        def w_vector_a(t, n):
-            mac(y2_rows4(t, n), y1_window(t, n, -1), tap(FW, 0, t), y2_rows4(t, n))
-
-        def w_vector_b(t, n):
-            mac(y2_rows4(t, n), y1_window(t, n, 1), tap(FW, 2, t), y2_rows4(t, n))
-
-        def d_scalar(t, n, rows=slice(0, ROWS)):
-            scaled(as_rows(y2d[t][n % 2], rows), y2_window(t, n, -1, rows), tap(FD, 0, t))
-
-        def d_vector_a(t, n, rows=slice(0, ROWS)):
-            acc = as_rows(y2d[t][n % 2], rows)
-            mac(acc, y2_window(t, n, 1, rows), tap(FD, 2, t), acc)
-
-        def d_vector_b(t, n, rows=slice(0, ROWS)):
-            mac(as_rows(y3[n % 2][:, t, :], rows), y2_window(t, n, 0, rows), tap(FD, 1, t), as_rows(y2d[t][n % 2], rows))
+        def two_tiles(steps, ts, *args):
+            for step in steps:
+                for t in ts:
+                    step(t, *args)
 
         def second_product(n, c0=0, c1=CHUNK):
             for m in range(PACK):
@@ -216,16 +224,16 @@ def tile_lowrankconv3d_kernel(tc, x, U_kh, U_kw, U_kd, U_c_in, U_c_out, bias, ou
                 nc.vector.tensor_scalar(out=res, in0=banks[("out", m, n, c0)], scalar1=bias_f[:, m : m + 1], scalar2=None, op0=ADD)
             nc.sync.dma_start(out=out_rows[:, m, n * CHUNK + c0 : n * CHUNK + c1], in_=res)
 
-        def each(steps, ts, *args):
-            for step in steps:
-                for t in ts:
-                    step(t, *args)
-
         nc.gpsimd.memset(warm, 0.0)
+        make_identity(nc, ident)
         for t in range(PACK):
-            nc.gpsimd.memset(y1[t].rearrange("p (s c) -> p s c", c=Y1_PITCH)[:, :, 0:D], 0.0)
+            nc.vector.memset(y1[t].rearrange("p (s c) -> p s c", c=Y1_PITCH)[:, :, 0:D], 0.0)
             for b in range(2):
-                nc.gpsimd.memset(y2[t][b].rearrange("p (r c) -> p r c", c=Y2_PITCH)[:, :, 0:4], 0.0)
+                nc.gpsimd.memset(y2[t][b].rearrange("p (r c) -> p r c", c=Y2_PITCH)[:, :, 0:Y2_PAD], 0.0)
+        for t in T_VE:
+            nc.vector.memset(slabs(t, 0, 1), 0.0)
+        nc.vector.memset(y0_pe[:, 0:SLAB], 0.0)
+        nc.vector.memset(y0_pe[:, (H + 1) * SLAB : (H + 2) * SLAB], 0.0)
 
         for f, u in enumerate((U_kh, U_kw, U_kd)):
             nc.scalar.dma_start(out=taps_bf[f], in_=u.rearrange("k (p t) -> p k t", t=PACK))
@@ -236,9 +244,6 @@ def tile_lowrankconv3d_kernel(tc, x, U_kh, U_kw, U_kd, U_c_in, U_c_out, bias, ou
             nc.sync.dma_start(out=x_raw[n], in_=x_rows[:, :, n * CHUNK : (n + 1) * CHUNK])
         nc.sync.dma_start(out=w_raw[1], in_=U_c_out.rearrange("(p j) r -> p j r", j=PACK))
 
-        nc.gpsimd.memset(y0[:, 0:SLAB], 0.0)
-        nc.gpsimd.memset(y0[:, (H + 1) * SLAB : (H + 2) * SLAB], 0.0)
-        make_identity(nc, ident)
         for f in range(3):
             nc.vector.tensor_copy(out=taps[:, f], in_=taps_bf[f])
         nc.vector.tensor_copy(out=bias_f, in_=bias_bf)
@@ -248,7 +253,7 @@ def tile_lowrankconv3d_kernel(tc, x, U_kh, U_kw, U_kd, U_c_in, U_c_out, bias, ou
         group_weight("V", 0, 0, PACK)
         group_x("S", 0, SLAB, CHUNK)
         group_x("V", 0, 0, SLAB)
-        quantize(w_codes[0], w_scales[0], w_grp[0])
+        quantize_weight(0)
         quantize_x(0)
         first_product(0)
         group_x("S", 1, SLAB, CHUNK)
@@ -259,83 +264,89 @@ def tile_lowrankconv3d_kernel(tc, x, U_kh, U_kw, U_kd, U_c_in, U_c_out, bias, ou
             group_x("G", n, 0, SLAB)
             group_x("G", n, SLAB, CHUNK)
 
-        each([h_scalar], T_VE, 0)
         for t in T_VE:
-            h_vector_first_a(t)
-            h_vector_a(t, 0)
-            h_vector_first_b(t)
-        h_scalar(0, 1)
+            h_lower(t, 0)
+        h_vector(0)
         h_copy_in(0)
         h_copy_in(1)
         h_tensor(0)
-        each([h_scalar], (1, 2), 1)
+        for t in T_VE:
+            h_lower(t, 1)
 
         for n in range(NCHUNK - 1):
+            h_vector(n + 1)
             for t in T_VE:
-                h_vector_a(t, n + 1)
-                h_vector_b(t, n + 1)
-            each([w_scalar], T_VE, n)
+                w_centre(t, n)
+            if n == 0:
+                quantize_x(2)
             if n + 2 < NCHUNK:
-                quantize_x(n + 2)
                 first_product(n + 2)
             h_copy_out(n)
-            w_scalar(T_PE, n)
-            each([w_vector_a, w_vector_b], (0, 1), n)
-            each([d_scalar], (0, 1), n)
+            w_centre(T_PE, n)
+            two_tiles((w_lower, w_upper), (0, 1), n)
+            two_tiles((d_lower,), (0, 1), n)
             if n + 2 < NCHUNK:
                 h_copy_in(n + 2)
             h_tensor(n + 1)
+            if n == 0:
+                quantize_x(3)
             if n == 1:
-                quantize(w_codes[1], w_scales[1], w_grp[1])
+                quantize_weight(1)
             if n >= 1:
                 quantize_y3(n - 1)
                 second_product(n - 1)
-            each([w_vector_a, w_vector_b], (2, 3), n)
-            each([d_scalar], (2, 3), n)
-            each([d_vector_a, d_vector_b], (0, 1), n)
+            two_tiles((w_lower, w_upper), (2, 3), n)
+            two_tiles((d_lower,), (2, 3), n)
+            two_tiles((d_upper, d_centre), (0, 1), n)
             if n + 2 < NCHUNK:
-                each([h_scalar], T_VE, n + 2)
+                for t in T_VE:
+                    h_lower(t, n + 2)
             else:
-                each([w_scalar], T_VE, n + 1)
+                for t in T_VE:
+                    w_centre(t, n + 1)
                 h_copy_out(n + 1)
-                w_scalar(T_PE, n + 1)
+                w_centre(T_PE, n + 1)
             for m in range(PACK):
                 if n == 0:
                     group_weight("S", 1, m, m + 1)
                 else:
                     store("S", m, n - 1)
-            each([d_vector_a, d_vector_b], (2, 3), n)
+            two_tiles((d_upper, d_centre), (2, 3), n)
             if n + 2 < NCHUNK:
-                group_y3("G", n, 0, 192)
-                group_y3("G", n, 192, 384)
-                group_y3("S", n, 384, CHUNK)
+                group_y3("G", n, 0, G_SHARE // 2)
+                group_y3("G", n, G_SHARE // 2, G_SHARE)
+                group_y3("S", n, G_SHARE, CHUNK)
 
         n = NCHUNK - 1
         top, bottom = slice(0, W), slice(W, ROWS)
         for q in range(4):
             group_y3("S", n - 1, q * SLAB // 2, (q + 1) * SLAB // 2)
-        each([w_vector_a, w_vector_b], (0, 1), n)
-        each([d_scalar], (0, 1), n, top)
-        each([w_vector_a, w_vector_b], (2, 3), n)
+        two_tiles((w_lower, w_upper), (0, 1), n)
+        two_tiles((d_lower,), (0, 1), n, top)
+        two_tiles((w_lower, w_upper), (2, 3), n)
         quantize_y3(n - 1)
         second_product(n - 1)
-        each([d_scalar], (2, 3), n, top)
-        each([d_vector_a, d_vector_b], (0, 1), n, top)
-        each([d_scalar], (0, 1, 2, 3), n, bottom)
-        each([d_vector_a, d_vector_b], (2, 3), n, top)
+        two_tiles((d_lower,), (2, 3), n, top)
+        two_tiles((d_upper, d_centre), (0, 1), n, top)
+        two_tiles((d_lower,), (0, 1, 2, 3), n, bottom)
+        two_tiles((d_upper, d_centre), (2, 3), n, top)
+        for m in (0, 1):
+            store("S", m, n - 1)
         group_y3("S", n, 0, SLAB // 2)
         group_y3("S", n, SLAB // 2, SLAB)
-        each([d_vector_a, d_vector_b], (0, 1), n, bottom)
-        for m in range(PACK):
+        two_tiles((d_upper, d_centre), (0, 1), n, bottom)
+        for m in (2, 3):
             store("S", m, n - 1)
-        each([d_vector_a], (2, 3), n, bottom)
+        two_tiles((d_upper,), (2, 3), n, bottom)
         quantize_y3(n, 0, SLAB)
         second_product(n, 0, SLAB)
-        each([d_vector_b], (2, 3), n, bottom)
-        for m in range(PACK):
+        two_tiles((d_centre,), (2, 3), n, bottom)
+        for m in (0, 1):
             store("S", m, n, 0, SLAB)
         group_y3("V", n, SLAB, CHUNK)
         quantize_y3(n, SLAB, CHUNK)
         second_product(n, SLAB, CHUNK)
+        for m in (2, 3):
+            store("V", m, n, 0, SLAB)
         for m in range(PACK):
             store("V" if m % 2 == 0 else "S", m, n, SLAB, CHUNK)

from contextlib import ExitStack

import concourse.mybir as mybir
from concourse.masks import make_identity

F32 = mybir.dt.float32
BF16 = mybir.dt.bfloat16
U32 = mybir.dt.uint32
U8 = mybir.dt.uint8
FP8X4 = mybir.dt.float8_e4m3fn_x4
MULT = mybir.AluOpType.mult
ADD = mybir.AluOpType.add
IDENT = mybir.ActivationFunctionType.Identity

BANK_DT = BF16

P = 128
PACK = 4
CIN, RANK, COUT = 512, 512, 512
H, W, D = 8, 16, 16
POS = H * W * D
SLAB = W * D
CHUNK = 2 * SLAB
NCHUNK = POS // CHUNK
Y1_PITCH = SLAB + D
Y1_SIZE = (H + 1) * Y1_PITCH
ROWS = CHUNK // D
Y2_PAD = 4
Y2_PITCH = D + Y2_PAD
Y2_SIZE = (ROWS + 1) * Y2_PITCH
FH, FW, FD = 0, 1, 2
T_VE = (0, 1, 2)
T_PE = 3
G_SHARE = 384

FLOPS = 2 * POS * RANK * (CIN + COUT) + 3 * 5 * POS * RANK


def tile_lowrankconv3d_kernel(tc, x, U_kh, U_kw, U_kd, U_c_in, U_c_out, bias, out):
    nc = tc.nc
    x_rows = x.rearrange("b c h w d -> (b c) (h w d)").rearrange("(p j) n -> p j n", j=PACK)
    out_rows = out.rearrange("b c h w d -> (b c) (h w d)").rearrange("(p m) n -> p m n", m=PACK)

    with ExitStack() as ctx:
        keep = ctx.enter_context(tc.tile_pool(name="keep", bufs=1))
        stage = ctx.enter_context(tc.tile_pool(name="stage", bufs=16))
        psum = ctx.enter_context(tc.psum_pool(name="psum", bufs=8))
        ctx.enter_context(tc.manual_schedule())

        def keep_tile(name, shape, dtype):
            return keep.tile(shape, dtype, name=name, tag=name, align_bytes=64)

        warm = keep_tile("warm", [P, 2], F32)
        taps_bf = [keep_tile("taps_bf%d" % f, [P, 3, PACK], BF16) for f in range(3)]
        bias_bf = keep_tile("bias_bf", [P, PACK], BF16)
        taps = keep_tile("taps", [P, 3, 3, PACK], F32)
        bias_f = keep_tile("bias_f", [P, PACK], F32)
        ident = keep_tile("ident", [P, P], F32)
        diag = [keep_tile("diag%d" % k, [P, P], BANK_DT) for k in range(3)]
        w_raw = [keep_tile("w_raw%d" % s, [P, PACK, 512], BF16) for s in range(2)]
        w_grp = [keep_tile("w_grp%d" % s, [P, PACK * 512], BF16) for s in range(2)]
        w_codes = [keep_tile("w_codes%d" % s, [P, 512], U32) for s in range(2)]
        w_scales = [keep_tile("w_scales%d" % s, [P, 512], U8) for s in range(2)]
        x_raw = [keep_tile("x_raw%d" % n, [P, PACK, CHUNK], BF16) for n in range(NCHUNK)]
        x_grp = [keep_tile("x_grp%d" % b, [P, CHUNK, PACK], BF16) for b in range(2)]
        x_codes = [keep_tile("x_codes%d" % n, [P, CHUNK], U32) for n in range(NCHUNK)]
        x_scales = [keep_tile("x_scales%d" % n, [P, CHUNK], U8) for n in range(NCHUNK)]
        y0_pe = keep_tile("y0_pe", [P, (H + 2) * SLAB], BANK_DT)
        y1 = [keep_tile("y1_%d" % t, [P, Y1_SIZE], F32) for t in range(PACK)]
        y2 = [[keep_tile("y2_%d_%d" % (t, b), [P, Y2_SIZE], F32) for b in range(2)] for t in range(PACK)]
        acc = [[keep_tile("acc_%d_%d" % (t, b), [P, CHUNK], F32) for b in range(2)] for t in range(PACK)]
        y3 = [keep_tile("y3_%d" % b, [P, PACK, CHUNK], BF16) for b in range(2)]
        y3_grp = [keep_tile("y3_grp%d" % b, [P, CHUNK, PACK], BF16) for b in range(2)]
        y3_codes = [keep_tile("y3_codes%d" % b, [P, CHUNK], U32) for b in range(2)]
        y3_scales = [keep_tile("y3_scales%d" % b, [P, CHUNK], U8) for b in range(2)]
        banks = {}

        def tap(f, k, t):
            return taps[:, f, k, t : t + 1]

        def slabs(t, h, count):
            start = D + h * Y1_PITCH
            return y1[t][:, start : start + count * Y1_PITCH].rearrange("p (s c) -> p s c", c=Y1_PITCH)[:, :, 0:SLAB]

        def bank_slabs(bank):
            return bank.rearrange("p (s c) -> p s c", c=SLAB)

        def y1_window(t, n, shift):
            start = D + 2 * n * Y1_PITCH + shift * D
            two = y1[t][:, start : start + 2 * Y1_PITCH].rearrange("p (s c) -> p s c", c=Y1_PITCH)[:, :, 0:SLAB]
            return two.rearrange("p s (w d) -> p s w d", d=D)

        def y2_window(t, n, shift, rows):
            start = Y2_PAD + shift
            view = y2[t][n % 2][:, start : start + ROWS * Y2_PITCH].rearrange("p (r c) -> p r c", c=Y2_PITCH)
            return view[:, rows, 0:D]

        def y2_chunk(t, n):
            return y2_window(t, n, 0, ALL_ROWS).rearrange("p (s w) d -> p s w d", s=2)

        def as_rows(ap, rows):
            return ap.rearrange("p (r d) -> p r d", d=D)[:, rows, :]

        ALL_ROWS = slice(0, ROWS)

        def scaled(out_ap, in_ap, scale_ap):
            nc.scalar.activation(out=out_ap, in_=in_ap, func=IDENT, bias=0.0, scale=scale_ap)

        def mac(out_ap, in_ap, scale_ap, acc_ap):
            nc.vector.scalar_tensor_tensor(out=out_ap, in0=in_ap, scalar=scale_ap, in1=acc_ap, op0=MULT, op1=ADD)

        def copy_on(engine, out_ap, in_ap):
            if engine == "V":
                nc.vector.tensor_copy(out=out_ap, in_=in_ap)
            elif engine == "S":
                nc.scalar.copy(out=out_ap, in_=in_ap)
            else:
                nc.gpsimd.tensor_scalar(out=out_ap, in0=in_ap, scalar1=1.0, scalar2=0.0, op0=MULT, op1=ADD)

        def group_weight(engine, s, t0, t1):
            dst = w_grp[s].rearrange("p (t m j) -> p t m j", t=PACK, j=PACK)
            src = w_raw[s].rearrange("p j (m t) -> p t m j", t=PACK)
            copy_on(engine, dst[:, t0:t1], src[:, t0:t1])

        def group_x(engine, n, c0, c1):
            copy_on(engine, x_grp[n % 2][:, c0:c1, :], x_raw[n].rearrange("p j c -> p c j")[:, c0:c1, :])

        def group_y3(engine, n, c0, c1):
            copy_on(engine, y3_grp[n % 2][:, c0:c1, :], y3[n % 2].rearrange("p t c -> p c t")[:, c0:c1, :])

        def quantize(codes, scales, grouped):
            nc.vector.quantize_mx(out=codes.bitcast(FP8X4), scales=scales, in_=grouped)

        def quantize_weight(s):
            quantize(w_codes[s], w_scales[s], w_grp[s])

        def quantize_x(n):
            quantize(x_codes[n], x_scales[n], x_grp[n % 2].rearrange("p c j -> p (c j)"))

        def quantize_y3(n, c0=0, c1=CHUNK):
            grouped = y3_grp[n % 2].rearrange("p c j -> p (c j)")
            quantize(y3_codes[n % 2][:, c0:c1], y3_scales[n % 2][:, c0:c1], grouped[:, PACK * c0 : PACK * c1])

        def product(dtype, s, m, codes, scales):
            bank = psum.tile([P, codes.shape[1]], dtype, name="bank", tag="bank")
            cols = slice(m * P, (m + 1) * P)
            nc.tensor.matmul_mx(
                out=bank,
                lhsT=w_codes[s][:, cols].bitcast(FP8X4),
                lhsT_scale=w_scales[s][:, cols],
                rhs=codes.bitcast(FP8X4),
                rhs_scale=scales,
                start=True,
                stop=True,
            )
            return bank

        def first_product(n):
            for t in T_VE + (T_PE,) if n == 0 else (T_PE,) + T_VE:
                banks[(t, n)] = product(BANK_DT, 0, t, x_codes[n], x_scales[n])

        def h_lower(t, n):
            count = 2 if n < NCHUNK - 1 else 1
            scaled(slabs(t, 2 * n + 1, count), bank_slabs(banks[(t, n)])[:, 0:count], tap(FH, 0, t))

        def h_centre(t, n):
            mac(slabs(t, 2 * n, 2), bank_slabs(banks[(t, n)]), tap(FH, 1, t), slabs(t, 2 * n, 2))

        def h_upper(t, n):
            first = 0 if n > 0 else 1
            dst = slabs(t, 2 * n - 1 + first, 2 - first)
            mac(dst, bank_slabs(banks[(t, n)])[:, first:2], tap(FH, 2, t), dst)

        def h_vector(n):
            for step in (h_centre, h_upper):
                for t in T_VE:
                    step(t, n)

        def h_copy_in(n):
            nc.scalar.copy(out=y0_pe[:, (2 * n + 1) * SLAB : (2 * n + 3) * SLAB], in_=banks[(T_PE, n)])

        def h_tensor(n):
            bank = psum.tile([P, CHUNK], F32, name="bank", tag="bank")
            for k in range(3):
                moving = y0_pe[:, (2 * n + k) * SLAB : (2 * n + k + 2) * SLAB]
                nc.tensor.matmul(out=bank, lhsT=diag[k], rhs=moving, start=(k == 0), stop=(k == 2))
            banks[("h", n)] = bank

        def h_copy_out(n):
            nc.scalar.copy(out=slabs(T_PE, 2 * n, 2), in_=bank_slabs(banks[("h", n)]))

        def w_centre(t, n):
            scaled(y2_chunk(t, n), y1_window(t, n, 0), tap(FW, 1, t))

        def w_lower(t, n):
            mac(y2_chunk(t, n), y1_window(t, n, -1), tap(FW, 0, t), y2_chunk(t, n))

        def w_upper(t, n):
            mac(y2_chunk(t, n), y1_window(t, n, 1), tap(FW, 2, t), y2_chunk(t, n))

        def d_lower(t, n, rows=ALL_ROWS):
            scaled(as_rows(acc[t][n % 2], rows), y2_window(t, n, -1, rows), tap(FD, 0, t))

        def d_upper(t, n, rows=ALL_ROWS):
            mac(as_rows(acc[t][n % 2], rows), y2_window(t, n, 1, rows), tap(FD, 2, t), as_rows(acc[t][n % 2], rows))

        def d_centre(t, n, rows=ALL_ROWS):
            mac(as_rows(y3[n % 2][:, t, :], rows), y2_window(t, n, 0, rows), tap(FD, 1, t), as_rows(acc[t][n % 2], rows))

        def two_tiles(steps, ts, *args):
            for step in steps:
                for t in ts:
                    step(t, *args)

        def second_product(n, c0=0, c1=CHUNK):
            for m in range(PACK):
                banks[("out", m, n, c0)] = product(F32, 1, m, y3_codes[n % 2][:, c0:c1], y3_scales[n % 2][:, c0:c1])

        def store(engine, m, n, c0=0, c1=CHUNK):
            res = stage.tile([P, c1 - c0], F32, name="res", tag="res")
            if engine == "S":
                nc.scalar.activation(out=res, in_=banks[("out", m, n, c0)], func=IDENT, bias=bias_f[:, m : m + 1], scale=1.0)
            else:
                nc.vector.tensor_scalar(out=res, in0=banks[("out", m, n, c0)], scalar1=bias_f[:, m : m + 1], scalar2=None, op0=ADD)
            nc.sync.dma_start(out=out_rows[:, m, n * CHUNK + c0 : n * CHUNK + c1], in_=res)

        nc.gpsimd.memset(warm, 0.0)
        make_identity(nc, ident)
        for t in range(PACK):
            nc.vector.memset(y1[t].rearrange("p (s c) -> p s c", c=Y1_PITCH)[:, :, 0:D], 0.0)
            for b in range(2):
                nc.gpsimd.memset(y2[t][b].rearrange("p (r c) -> p r c", c=Y2_PITCH)[:, :, 0:Y2_PAD], 0.0)
        for t in T_VE:
            nc.vector.memset(slabs(t, 0, 1), 0.0)
        nc.vector.memset(y0_pe[:, 0:SLAB], 0.0)
        nc.vector.memset(y0_pe[:, (H + 1) * SLAB : (H + 2) * SLAB], 0.0)

        for f, u in enumerate((U_kh, U_kw, U_kd)):
            nc.scalar.dma_start(out=taps_bf[f], in_=u.rearrange("k (p t) -> p k t", t=PACK))
        nc.scalar.dma_start(out=bias_bf, in_=bias.rearrange("(p m) -> p m", m=PACK))
        nc.scalar.activation(out=warm[:, 1:2], in_=warm[:, 0:1], func=IDENT, bias=0.0, scale=1.0)
        nc.sync.dma_start(out=w_raw[0], in_=U_c_in.rearrange("(p j) r -> p j r", j=PACK))
        for n in range(NCHUNK):
            nc.sync.dma_start(out=x_raw[n], in_=x_rows[:, :, n * CHUNK : (n + 1) * CHUNK])
        nc.sync.dma_start(out=w_raw[1], in_=U_c_out.rearrange("(p j) r -> p j r", j=PACK))

        for f in range(3):
            nc.vector.tensor_copy(out=taps[:, f], in_=taps_bf[f])
        nc.vector.tensor_copy(out=bias_f, in_=bias_bf)
        for k in range(3):
            scaled(diag[k], ident, tap(FH, k, T_PE))

        group_weight("V", 0, 0, PACK)
        group_x("S", 0, SLAB, CHUNK)
        group_x("V", 0, 0, SLAB)
        quantize_weight(0)
        quantize_x(0)
        first_product(0)
        group_x("S", 1, SLAB, CHUNK)
        group_x("V", 1, 0, SLAB)
        quantize_x(1)
        first_product(1)
        for n in (3, 2):
            group_x("G", n, 0, SLAB)
            group_x("G", n, SLAB, CHUNK)

        for t in T_VE:
            h_lower(t, 0)
        h_vector(0)
        h_copy_in(0)
        h_copy_in(1)
        h_tensor(0)
        for t in T_VE:
            h_lower(t, 1)

        for n in range(NCHUNK - 1):
            h_vector(n + 1)
            for t in T_VE:
                w_centre(t, n)
            if n == 0:
                quantize_x(2)
            if n + 2 < NCHUNK:
                first_product(n + 2)
            h_copy_out(n)
            w_centre(T_PE, n)
            two_tiles((w_lower, w_upper), (0, 1), n)
            two_tiles((d_lower,), (0, 1), n)
            if n + 2 < NCHUNK:
                h_copy_in(n + 2)
            h_tensor(n + 1)
            if n == 0:
                quantize_x(3)
            if n == 1:
                quantize_weight(1)
            if n >= 1:
                quantize_y3(n - 1)
                second_product(n - 1)
            two_tiles((w_lower, w_upper), (2, 3), n)
            two_tiles((d_lower,), (2, 3), n)
            two_tiles((d_upper, d_centre), (0, 1), n)
            if n + 2 < NCHUNK:
                for t in T_VE:
                    h_lower(t, n + 2)
            else:
                for t in T_VE:
                    w_centre(t, n + 1)
                h_copy_out(n + 1)
                w_centre(T_PE, n + 1)
            for m in range(PACK):
                if n == 0:
                    group_weight("S", 1, m, m + 1)
                else:
                    store("S", m, n - 1)
            two_tiles((d_upper, d_centre), (2, 3), n)
            if n + 2 < NCHUNK:
                group_y3("G", n, 0, G_SHARE // 2)
                group_y3("G", n, G_SHARE // 2, G_SHARE)
                group_y3("S", n, G_SHARE, CHUNK)

        n = NCHUNK - 1
        top, bottom = slice(0, W), slice(W, ROWS)
        for q in range(4):
            group_y3("S", n - 1, q * SLAB // 2, (q + 1) * SLAB // 2)
        two_tiles((w_lower, w_upper), (0, 1), n)
        two_tiles((d_lower,), (0, 1), n, top)
        two_tiles((w_lower, w_upper), (2, 3), n)
        quantize_y3(n - 1)
        second_product(n - 1)
        two_tiles((d_lower,), (2, 3), n, top)
        two_tiles((d_upper, d_centre), (0, 1), n, top)
        two_tiles((d_lower,), (0, 1, 2, 3), n, bottom)
        two_tiles((d_upper, d_centre), (2, 3), n, top)
        for m in (0, 1):
            store("S", m, n - 1)
        group_y3("S", n, 0, SLAB // 2)
        group_y3("S", n, SLAB // 2, SLAB)
        two_tiles((d_upper, d_centre), (0, 1), n, bottom)
        for m in (2, 3):
            store("S", m, n - 1)
        two_tiles((d_upper,), (2, 3), n, bottom)
        quantize_y3(n, 0, SLAB)
        second_product(n, 0, SLAB)
        two_tiles((d_centre,), (2, 3), n, bottom)
        for m in (0, 1):
            store("S", m, n, 0, SLAB)
        group_y3("V", n, SLAB, CHUNK)
        quantize_y3(n, SLAB, CHUNK)
        second_product(n, SLAB, CHUNK)
        for m in (2, 3):
            store("V", m, n, 0, SLAB)
        for m in range(PACK):
            store("V" if m % 2 == 0 else "S", m, n, SLAB, CHUNK)
